import numpy as np
import ml_dtypes


def mxq(x, axis, fmt="e4m3"):
    dtype, down = {"e4m3": (ml_dtypes.float8_e4m3fn, 7), "e5m2": (ml_dtypes.float8_e5m2, 14)}[fmt]
    v = np.moveaxis(np.asarray(x, np.float32).astype(ml_dtypes.bfloat16).astype(np.float64), axis, -1)
    blocks = v.reshape(v.shape[:-1] + (-1, 32))
    amax = np.abs(blocks).max(-1, keepdims=True)
    byte = np.maximum(np.where(amax > 0, np.frexp(amax)[1] - 1 + 127, 0) - down, 1)
    scale = np.exp2(byte - 127.0)
    codes = (blocks / scale).astype(np.float32).astype(dtype).astype(np.float64)
    return np.moveaxis((codes * scale).reshape(v.shape), -1, axis)


WIDE = False


def mx_kscale(k):
    if not WIDE:
        return np.ones(k)
    levels = np.array([20, -20, 10, -10, 0])
    a = np.random.permutation(np.resize(levels, k // 512 * 4)).reshape(k // 512, 4)
    idx = np.arange(k)
    return np.exp2(a[idx // 512, idx % 128 // 32])


BF16 = ml_dtypes.bfloat16


def bf(x):
    return np.asarray(x, np.float32).astype(BF16)


def f64(x):
    return np.asarray(x).astype(np.float64)


B, HH, WW, E, NH, D = 1, 128, 4, 8192, 8, 128
KD = NH * D


def setup_inputs():
    u = mx_kscale(E)
    ret_w = np.random.standard_normal((B, HH, WW, NH, D)) * 0.9
    kv_h = np.random.standard_normal((B, WW, NH, D, D)) * 0.8
    Wo = np.random.standard_normal((E, KD)) * 0.3 / np.sqrt(KD) / u[:, None]
    bo = np.random.standard_normal(E) * 0.2
    g = np.random.standard_normal((B, HH * WW, E)) * np.exp2(np.random.randint(-12, 1, (B, HH * WW, 1))) * 8.0 * u
    return {"ret_w": bf(ret_w), "kv_h": bf(kv_h), "Wo": bf(Wo), "bo": bf(bo), "grad_out": bf(g)}


def reference(ret_w, kv_h, Wo, bo, grad_out):
    g = f64(grad_out).reshape(B * HH * WW, E)
    go = mxq(g, 1, "e5m2") @ mxq(f64(Wo), 0, "e4m3")
    go = go.reshape(B, HH, WW * NH, D).transpose(0, 2, 1, 3)
    gr = go @ f64(kv_h).reshape(B, WW * NH, D, D).transpose(0, 1, 3, 2)
    return gr.transpose(0, 2, 1, 3).reshape(B, HH, WW, NH, D)

@@ -1,0 +1,189 @@
+from contextlib import ExitStack
+
+import concourse.mybir as mybir
+from concourse.masks import make_identity
+
+F32 = mybir.dt.float32
+BF16 = mybir.dt.bfloat16
+U32 = mybir.dt.uint32
+U8 = mybir.dt.uint8
+E4M3_X4 = mybir.dt.float8_e4m3fn_x4
+E5M2_X4 = mybir.dt.float8_e5m2_x4
+
+P = 128
+PACK = 4
+K_PASS = P * PACK
+HEIGHT, WIDTH, HEADS, D = 128, 4, 8, 128
+TOKENS = HEIGHT * WIDTH
+CHANNELS = 8192
+KD = HEADS * D
+PASSES = CHANNELS // K_PASS
+BANK_F32 = 512
+KV_ROWS = 32
+W_AHEAD = 6
+
+FLOPS = 2 * TOKENS * CHANNELS * KD + 2 * WIDTH * HEADS * HEIGHT * D * D
+
+
+def tile_linear_retention_pb_k_kernel(tc, ret_w, kv_h, Wo, bo, grad_out, out):
+    nc = tc.nc
+
+    g_tiles = grad_out.rearrange("b (h w) k -> (b w) h k", w=WIDTH)
+    w_passes = Wo.rearrange("(g u q e) c -> g q u (e c)", u=2, q=P, e=2)
+    kv_rows = kv_h.rearrange("b w n (a i) f -> (b w n a) i f", i=KV_ROWS)
+    out_rows = out.rearrange("b h w n e -> (b h) w (n e)")
+
+    def copy_on(use_vector, dst, src):
+        if use_vector:
+            nc.vector.tensor_copy(out=dst, in_=src)
+        else:
+            nc.scalar.copy(out=dst, in_=src)
+
+    with ExitStack() as ctx:
+        ctx.enter_context(tc.manual_schedule())
+        keep = ctx.enter_context(tc.tile_pool(name="keep", bufs=1))
+        big = ctx.enter_context(tc.tile_pool(name="big", bufs=WIDTH))
+        w_in = ctx.enter_context(tc.tile_pool(name="w_in", bufs=W_AHEAD))
+        g_stage = ctx.enter_context(tc.tile_pool(name="g_stage", bufs=4))
+        w_stage = ctx.enter_context(tc.tile_pool(name="w_stage", bufs=3))
+        w_quant = ctx.enter_context(tc.tile_pool(name="w_quant", bufs=3))
+        psum = ctx.enter_context(tc.psum_pool(name="psum", bufs=8))
+
+        kv_raw = keep.tile([P, KV_ROWS, D], BF16)
+        nc.sync.dma_start(out=kv_raw[:], in_=kv_rows)
+        g_raw = []
+        for w in range(WIDTH):
+            g_raw.append(big.tile([P, CHANNELS], BF16, name="g_raw%d" % w, tag="big"))
+            nc.sync.dma_start(out=g_raw[w][:], in_=g_tiles[w, :, :])
+
+        w_raw = {}
+
+        def load_w(c):
+            w_raw[c] = w_in.tile([P, PACK, KD], BF16, name="w_raw%d" % c, tag="w_raw")
+            nc.sync.dma_start(
+                out=w_raw[c][:].rearrange("q (u e) c -> q u (e c)", u=2), in_=w_passes[c, :, :, :]
+            )
+
+        for c in range(W_AHEAD):
+            load_w(c)
+
+        ident_f32 = keep.tile([P, P], F32)
+        make_identity(nc, ident_f32[:])
+        ident_bf16 = keep.tile([P, P], BF16)
+        make_identity(nc, ident_bf16[:])
+
+        kv_t = keep.tile([P, P, KV_ROWS], F32)
+        kv_per_bank = 8
+        for b in range(KV_ROWS // kv_per_bank):
+            kv_bank = psum.tile([P, kv_per_bank, P], BF16, tag="bank")
+            for j in range(kv_per_bank):
+                nc.tensor.transpose(kv_bank[:, j, :], kv_raw[:, b * kv_per_bank + j, :], ident_bf16[:])
+            copy_on(
+                b % 2 == 1,
+                kv_t[:, :, b * kv_per_bank : (b + 1) * kv_per_bank],
+                kv_bank[:].rearrange("f j p -> f p j"),
+            )
+        kv_cols = kv_t[:].rearrange("f p i -> f (p i)")
+
+        g_codes = keep.tile([P, PASSES, TOKENS], U32, align_bytes=64)
+        g_scales = keep.tile([P, PASSES, TOKENS], U8, align_bytes=64)
+
+        def quantise_g(w, pair, grouped):
+            for s in range(2):
+                g = 2 * pair + s
+                nc.vector.quantize_mx(
+                    out=g_codes[:, g, w * P : (w + 1) * P].bitcast(E5M2_X4),
+                    scales=g_scales[:, g, w * P : (w + 1) * P],
+                    in_=grouped[:, s * K_PASS : (s + 1) * K_PASS],
+                )
+
+        waiting = None
+        for w in range(WIDTH):
+            words = g_raw[w][:].bitcast(F32)
+            for pair in range(PASSES // 2):
+                bank = psum.tile([P, 2, 2, P], F32, tag="bank")
+                for s in range(2):
+                    for u in range(2):
+                        first = (2 * pair + s) * (K_PASS // 2) + u * P
+                        nc.tensor.transpose(bank[:, s, u, :], words[:, first : first + P], ident_f32[:])
+                grouped = g_stage.tile([P, 2 * K_PASS], BF16, align_bytes=64)
+                copy_on(
+                    pair % 4 == 3,
+                    grouped[:].bitcast(F32).rearrange("p (s h u) -> p s h u", s=2, u=2),
+                    bank[:].rearrange("p s u h -> p s h u"),
+                )
+                if waiting is not None:
+                    quantise_g(*waiting)
+                waiting = (w, pair, grouped)
+        quantise_g(*waiting)
+
+        half = KD // 2
+        w_grouped = {}
+
+        def regroup_w(c):
+            tiles = []
+            for side in range(2):
+                grouped = w_stage.tile(
+                    [P, half, PACK], BF16, name="w_grouped%d_%d" % (c, side), tag="side%d" % side, align_bytes=64
+                )
+                copy_on(
+                    side == 0,
+                    grouped[:].rearrange("q (c i) t -> q c t i", i=4),
+                    w_raw[c][:, :, side * half : (side + 1) * half].rearrange("q t (c i) -> q c t i", i=4),
+                )
+                tiles.append(grouped)
+            w_grouped[c] = tiles
+
+        acc = [psum.tile([P, TOKENS], F32, name="acc%d" % n, tag="bank") for n in range(HEADS)]
+
+        regroup_w(0)
+        for c in range(PASSES):
+            if c + 1 < PASSES:
+                regroup_w(c + 1)
+            w_codes = w_quant.tile([P, KD], U32, align_bytes=64)
+            w_scales = w_quant.tile([P, KD], U8, align_bytes=64)
+            for side in range(2):
+                cols = slice(side * half, (side + 1) * half)
+                nc.vector.quantize_mx(
+                    out=w_codes[:, cols].bitcast(E4M3_X4),
+                    scales=w_scales[:, cols],
+                    in_=w_grouped[c][side][:].rearrange("q c t -> q (c t)"),
+                )
+            if c + W_AHEAD < PASSES:
+                load_w(c + W_AHEAD)
+            for n in range(HEADS):
+                cols = slice(n * D, (n + 1) * D)
+                nc.tensor.matmul_mx(
+                    out=acc[n][:],
+                    lhsT=w_codes[:, cols].bitcast(E4M3_X4),
+                    lhsT_scale=w_scales[:, cols],
+                    rhs=g_codes[:, c, :].bitcast(E5M2_X4),
+                    rhs_scale=g_scales[:, c, :],
+                    start=(c == 0),
+                    stop=(c == PASSES - 1),
+                )
+
+        go2_t = big.tile([P, HEADS, TOKENS], F32, tag="big")
+        for n in range(HEADS):
+            copy_on(n % 2 == 1, go2_t[:, n, :], acc[n][:])
+
+        out_sb = big.tile([P, WIDTH, KD], F32, tag="big")
+        heads_per_bank = BANK_F32 // D
+        for w in range(WIDTH):
+            for b in range(HEADS // heads_per_bank):
+                out_bank = psum.tile([P, heads_per_bank, D], F32, tag="bank")
+                for j in range(heads_per_bank):
+                    n = b * heads_per_bank + j
+                    nc.tensor.matmul(
+                        out=out_bank[:, j, :],
+                        lhsT=go2_t[:, n, w * HEIGHT : (w + 1) * HEIGHT],
+                        rhs=kv_cols[:, (w * HEADS + n) * D : (w * HEADS + n + 1) * D],
+                        start=True,
+                        stop=True,
+                    )
+                copy_on(
+                    b % 2 == 1,
+                    out_sb[:, w, b * BANK_F32 : (b + 1) * BANK_F32],
+                    out_bank[:].rearrange("h n e -> h (n e)"),
+                )
+            nc.sync.dma_start(out=out_rows[:, w, :], in_=out_sb[:, w, :])

@@ -21,6 +21,8 @@ PASSES = CHANNELS // K_PASS
 BANK_F32 = 512
 KV_ROWS = 32
 W_AHEAD = 6
+G_PIECES = 2
+QUARTER = KD // 4
 
 FLOPS = 2 * TOKENS * CHANNELS * KD + 2 * WIDTH * HEADS * HEIGHT * D * D
 
@@ -45,7 +47,7 @@ def tile_linear_retention_pb_k_kernel(tc, ret_w, kv_h, Wo, bo, grad_out, out):
         big = ctx.enter_context(tc.tile_pool(name="big", bufs=WIDTH))
         w_in = ctx.enter_context(tc.tile_pool(name="w_in", bufs=W_AHEAD))
         g_stage = ctx.enter_context(tc.tile_pool(name="g_stage", bufs=4))
-        w_stage = ctx.enter_context(tc.tile_pool(name="w_stage", bufs=3))
+        w_stage = ctx.enter_context(tc.tile_pool(name="w_stage", bufs=12))
         w_quant = ctx.enter_context(tc.tile_pool(name="w_quant", bufs=3))
         psum = ctx.enter_context(tc.psum_pool(name="psum", bufs=8))
 
@@ -54,7 +56,9 @@ def tile_linear_retention_pb_k_kernel(tc, ret_w, kv_h, Wo, bo, grad_out, out):
         g_raw = []
         for w in range(WIDTH):
             g_raw.append(big.tile([P, CHANNELS], BF16, name="g_raw%d" % w, tag="big"))
-            nc.sync.dma_start(out=g_raw[w][:], in_=g_tiles[w, :, :])
+            for piece in range(G_PIECES):
+                cols = slice(piece * CHANNELS // G_PIECES, (piece + 1) * CHANNELS // G_PIECES)
+                nc.sync.dma_start(out=g_raw[w][:, cols], in_=g_tiles[w, :, cols])
 
         w_raw = {}
 
@@ -117,40 +121,31 @@ def tile_linear_retention_pb_k_kernel(tc, ret_w, kv_h, Wo, bo, grad_out, out):
                 waiting = (w, pair, grouped)
         quantise_g(*waiting)
 
-        half = KD // 2
-        w_grouped = {}
-
-        def regroup_w(c):
-            tiles = []
-            for side in range(2):
-                grouped = w_stage.tile(
-                    [P, half, PACK], BF16, name="w_grouped%d_%d" % (c, side), tag="side%d" % side, align_bytes=64
-                )
-                copy_on(
-                    side == 0,
-                    grouped[:].rearrange("q (c i) t -> q c t i", i=4),
-                    w_raw[c][:, :, side * half : (side + 1) * half].rearrange("q t (c i) -> q c t i", i=4),
-                )
-                tiles.append(grouped)
-            w_grouped[c] = tiles
-
         acc = [psum.tile([P, TOKENS], F32, name="acc%d" % n, tag="bank") for n in range(HEADS)]
 
-        regroup_w(0)
         for c in range(PASSES):
-            if c + 1 < PASSES:
-                regroup_w(c + 1)
+            w_grouped = []
+            for j in range(4):
+                grouped = w_stage.tile(
+                    [P, QUARTER, PACK], BF16, name="w_grouped%d_%d" % (c, j), tag="w_grouped", align_bytes=64
+                )
+                copy_on(
+                    j < 2,
+                    grouped[:].rearrange("q (c i) t -> q c t i", i=4),
+                    w_raw[c][:, :, j * QUARTER : (j + 1) * QUARTER].rearrange("q t (c i) -> q c t i", i=4),
+                )
+                w_grouped.append(grouped)
+            if c + W_AHEAD < PASSES:
+                load_w(c + W_AHEAD)
             w_codes = w_quant.tile([P, KD], U32, align_bytes=64)
             w_scales = w_quant.tile([P, KD], U8, align_bytes=64)
-            for side in range(2):
-                cols = slice(side * half, (side + 1) * half)
+            for j in range(4):
+                cols = slice(j * QUARTER, (j + 1) * QUARTER)
                 nc.vector.quantize_mx(
                     out=w_codes[:, cols].bitcast(E4M3_X4),
                     scales=w_scales[:, cols],
-                    in_=w_grouped[c][side][:].rearrange("q c t -> q (c t)"),
+                    in_=w_grouped[j][:].rearrange("q c t -> q (c t)"),
                 )
-            if c + W_AHEAD < PASSES:
-                load_w(c + W_AHEAD)
             for n in range(HEADS):
                 cols = slice(n * D, (n + 1) * D)
                 nc.tensor.matmul_mx(
@@ -181,9 +176,6 @@ def tile_linear_retention_pb_k_kernel(tc, ret_w, kv_h, Wo, bo, grad_out, out):
                         start=True,
                         stop=True,
                     )
-                copy_on(
-                    b % 2 == 1,
-                    out_sb[:, w, b * BANK_F32 : (b + 1) * BANK_F32],
-                    out_bank[:].rearrange("h n e -> h (n e)"),
-                )
-            nc.sync.dma_start(out=out_rows[:, w, :], in_=out_sb[:, w, :])
+                cols = slice(b * BANK_F32, (b + 1) * BANK_F32)
+                copy_on(b % 2 == 1, out_sb[:, w, cols], out_bank[:].rearrange("h n e -> h (n e)"))
+                nc.sync.dma_start(out=out_rows[:, w, cols], in_=out_sb[:, w, cols])

@@ -21,8 +21,8 @@ PASSES = CHANNELS // K_PASS
 BANK_F32 = 512
 KV_ROWS = 32
 W_AHEAD = 6
-G_PIECES = 2
-QUARTER = KD // 4
+G_PIECES = (2, 2, 2, 4)
+HALF = KD // 2
 
 FLOPS = 2 * TOKENS * CHANNELS * KD + 2 * WIDTH * HEADS * HEIGHT * D * D
 
@@ -46,8 +46,8 @@ def tile_linear_retention_pb_k_kernel(tc, ret_w, kv_h, Wo, bo, grad_out, out):
         keep = ctx.enter_context(tc.tile_pool(name="keep", bufs=1))
         big = ctx.enter_context(tc.tile_pool(name="big", bufs=WIDTH))
         w_in = ctx.enter_context(tc.tile_pool(name="w_in", bufs=W_AHEAD))
-        g_stage = ctx.enter_context(tc.tile_pool(name="g_stage", bufs=4))
-        w_stage = ctx.enter_context(tc.tile_pool(name="w_stage", bufs=12))
+        g_stage = ctx.enter_context(tc.tile_pool(name="g_stage", bufs=5))
+        w_stage = ctx.enter_context(tc.tile_pool(name="w_stage", bufs=5))
         w_quant = ctx.enter_context(tc.tile_pool(name="w_quant", bufs=3))
         psum = ctx.enter_context(tc.psum_pool(name="psum", bufs=8))
 
@@ -56,8 +56,8 @@ def tile_linear_retention_pb_k_kernel(tc, ret_w, kv_h, Wo, bo, grad_out, out):
         g_raw = []
         for w in range(WIDTH):
             g_raw.append(big.tile([P, CHANNELS], BF16, name="g_raw%d" % w, tag="big"))
-            for piece in range(G_PIECES):
-                cols = slice(piece * CHANNELS // G_PIECES, (piece + 1) * CHANNELS // G_PIECES)
+            for piece in range(G_PIECES[w]):
+                cols = slice(piece * CHANNELS // G_PIECES[w], (piece + 1) * CHANNELS // G_PIECES[w])
                 nc.sync.dma_start(out=g_raw[w][:, cols], in_=g_tiles[w, :, cols])
 
         w_raw = {}
@@ -123,40 +123,57 @@ def tile_linear_retention_pb_k_kernel(tc, ret_w, kv_h, Wo, bo, grad_out, out):
 
         acc = [psum.tile([P, TOKENS], F32, name="acc%d" % n, tag="bank") for n in range(HEADS)]
 
-        for c in range(PASSES):
-            w_grouped = []
-            for j in range(4):
-                grouped = w_stage.tile(
-                    [P, QUARTER, PACK], BF16, name="w_grouped%d_%d" % (c, j), tag="w_grouped", align_bytes=64
-                )
-                copy_on(
-                    j < 2,
-                    grouped[:].rearrange("q (c i) t -> q c t i", i=4),
-                    w_raw[c][:, :, j * QUARTER : (j + 1) * QUARTER].rearrange("q t (c i) -> q c t i", i=4),
-                )
-                w_grouped.append(grouped)
-            if c + W_AHEAD < PASSES:
-                load_w(c + W_AHEAD)
-            w_codes = w_quant.tile([P, KD], U32, align_bytes=64)
-            w_scales = w_quant.tile([P, KD], U8, align_bytes=64)
-            for j in range(4):
-                cols = slice(j * QUARTER, (j + 1) * QUARTER)
-                nc.vector.quantize_mx(
-                    out=w_codes[:, cols].bitcast(E4M3_X4),
-                    scales=w_scales[:, cols],
-                    in_=w_grouped[j][:].rearrange("q c t -> q (c t)"),
-                )
-            for n in range(HEADS):
+        w_grouped = {}
+        w_codes = {}
+        w_scales = {}
+
+        def regroup_w(c, half):
+            grouped = w_stage.tile(
+                [P, HALF, PACK], BF16, name="w_grouped%d_%d" % (c, half), tag="w_grouped", align_bytes=64
+            )
+            copy_on(
+                half == 0,
+                grouped[:].rearrange("q (c i) t -> q c t i", i=4),
+                w_raw[c][:, :, half * HALF : (half + 1) * HALF].rearrange("q t (c i) -> q c t i", i=4),
+            )
+            w_grouped[c, half] = grouped
+
+        def quantise_w(c, half):
+            if half == 0:
+                w_codes[c] = w_quant.tile([P, KD], U32, name="w_codes%d" % c, tag="w_codes", align_bytes=64)
+                w_scales[c] = w_quant.tile([P, KD], U8, name="w_scales%d" % c, tag="w_scales", align_bytes=64)
+            cols = slice(half * HALF, (half + 1) * HALF)
+            nc.vector.quantize_mx(
+                out=w_codes[c][:, cols].bitcast(E4M3_X4),
+                scales=w_scales[c][:, cols],
+                in_=w_grouped[c, half][:].rearrange("q c t -> q (c t)"),
+            )
+
+        def multiply(c, half):
+            for n in range(half * HEADS // 2, (half + 1) * HEADS // 2):
                 cols = slice(n * D, (n + 1) * D)
                 nc.tensor.matmul_mx(
                     out=acc[n][:],
-                    lhsT=w_codes[:, cols].bitcast(E4M3_X4),
-                    lhsT_scale=w_scales[:, cols],
+                    lhsT=w_codes[c][:, cols].bitcast(E4M3_X4),
+                    lhsT_scale=w_scales[c][:, cols],
                     rhs=g_codes[:, c, :].bitcast(E5M2_X4),
                     rhs_scale=g_scales[:, c, :],
                     start=(c == 0),
                     stop=(c == PASSES - 1),
                 )
+
+        for c in range(PASSES):
+            regroup_w(c, 0)
+            regroup_w(c, 1)
+            if c + W_AHEAD < PASSES:
+                load_w(c + W_AHEAD)
+            if c > 0:
+                quantise_w(c - 1, 1)
+                multiply(c - 1, 1)
+            quantise_w(c, 0)
+            multiply(c, 0)
+        quantise_w(PASSES - 1, 1)
+        multiply(PASSES - 1, 1)
 
         go2_t = big.tile([P, HEADS, TOKENS], F32, tag="big")
         for n in range(HEADS):
@@ -164,8 +181,8 @@ def tile_linear_retention_pb_k_kernel(tc, ret_w, kv_h, Wo, bo, grad_out, out):
 
         out_sb = big.tile([P, WIDTH, KD], F32, tag="big")
         heads_per_bank = BANK_F32 // D
-        for w in range(WIDTH):
-            for b in range(HEADS // heads_per_bank):
+        for b in range(HEADS // heads_per_bank):
+            for w in range(WIDTH):
                 out_bank = psum.tile([P, heads_per_bank, D], F32, tag="bank")
                 for j in range(heads_per_bank):
                     n = b * heads_per_bank + j
@@ -177,5 +194,5 @@ def tile_linear_retention_pb_k_kernel(tc, ret_w, kv_h, Wo, bo, grad_out, out):
                         stop=True,
                     )
                 cols = slice(b * BANK_F32, (b + 1) * BANK_F32)
-                copy_on(b % 2 == 1, out_sb[:, w, cols], out_bank[:].rearrange("h n e -> h (n e)"))
+                copy_on(w % 2 == 1, out_sb[:, w, cols], out_bank[:].rearrange("h n e -> h (n e)"))
                 nc.sync.dma_start(out=out_rows[:, w, cols], in_=out_sb[:, w, cols])

@@ -23,6 +23,7 @@ KV_ROWS = 32
 W_AHEAD = 6
 G_PIECES = (2, 2, 2, 4)
 HALF = KD // 2
+VECTOR_COLS = 480
 
 FLOPS = 2 * TOKENS * CHANNELS * KD + 2 * WIDTH * HEADS * HEIGHT * D * D
 
@@ -47,7 +48,7 @@ def tile_linear_retention_pb_k_kernel(tc, ret_w, kv_h, Wo, bo, grad_out, out):
         big = ctx.enter_context(tc.tile_pool(name="big", bufs=WIDTH))
         w_in = ctx.enter_context(tc.tile_pool(name="w_in", bufs=W_AHEAD))
         g_stage = ctx.enter_context(tc.tile_pool(name="g_stage", bufs=5))
-        w_stage = ctx.enter_context(tc.tile_pool(name="w_stage", bufs=5))
+        w_stage = ctx.enter_context(tc.tile_pool(name="w_stage", bufs=3))
         w_quant = ctx.enter_context(tc.tile_pool(name="w_quant", bufs=3))
         psum = ctx.enter_context(tc.psum_pool(name="psum", bufs=8))
 
@@ -127,16 +128,19 @@ def tile_linear_retention_pb_k_kernel(tc, ret_w, kv_h, Wo, bo, grad_out, out):
         w_codes = {}
         w_scales = {}
 
-        def regroup_w(c, half):
-            grouped = w_stage.tile(
-                [P, HALF, PACK], BF16, name="w_grouped%d_%d" % (c, half), tag="w_grouped", align_bytes=64
-            )
-            copy_on(
-                half == 0,
-                grouped[:].rearrange("q (c i) t -> q c t i", i=4),
-                w_raw[c][:, :, half * HALF : (half + 1) * HALF].rearrange("q t (c i) -> q c t i", i=4),
-            )
-            w_grouped[c, half] = grouped
+        def regroup_w(c):
+            grouped = w_stage.tile([P, KD, PACK], BF16, name="w_grouped%d" % c, tag="w_grouped", align_bytes=64)
+            for use_vector, cols in (
+                (False, slice(VECTOR_COLS, HALF)),
+                (True, slice(0, VECTOR_COLS)),
+                (False, slice(HALF, KD)),
+            ):
+                copy_on(
+                    use_vector,
+                    grouped[:, cols, :].rearrange("q (c i) t -> q c t i", i=4),
+                    w_raw[c][:, :, cols].rearrange("q t (c i) -> q c t i", i=4),
+                )
+            w_grouped[c] = grouped
 
         def quantise_w(c, half):
             if half == 0:
@@ -146,7 +150,7 @@ def tile_linear_retention_pb_k_kernel(tc, ret_w, kv_h, Wo, bo, grad_out, out):
             nc.vector.quantize_mx(
                 out=w_codes[c][:, cols].bitcast(E4M3_X4),
                 scales=w_scales[c][:, cols],
-                in_=w_grouped[c, half][:].rearrange("q c t -> q (c t)"),
+                in_=w_grouped[c][:, cols, :].rearrange("q c t -> q (c t)"),
             )
 
         def multiply(c, half):
@@ -163,8 +167,7 @@ def tile_linear_retention_pb_k_kernel(tc, ret_w, kv_h, Wo, bo, grad_out, out):
                 )
 
         for c in range(PASSES):
-            regroup_w(c, 0)
-            regroup_w(c, 1)
+            regroup_w(c)
             if c + W_AHEAD < PASSES:
                 load_w(c + W_AHEAD)
             if c > 0:

@@ -23,7 +23,8 @@ KV_ROWS = 32
 W_AHEAD = 6
 G_PIECES = (2, 2, 2, 4)
 HALF = KD // 2
-VECTOR_COLS = 480
+VECTOR_COLS = 240
+LATE_PAIRS = 2
 
 FLOPS = 2 * TOKENS * CHANNELS * KD + 2 * WIDTH * HEADS * HEIGHT * D * D
 
@@ -48,7 +49,7 @@ def tile_linear_retention_pb_k_kernel(tc, ret_w, kv_h, Wo, bo, grad_out, out):
         big = ctx.enter_context(tc.tile_pool(name="big", bufs=WIDTH))
         w_in = ctx.enter_context(tc.tile_pool(name="w_in", bufs=W_AHEAD))
         g_stage = ctx.enter_context(tc.tile_pool(name="g_stage", bufs=5))
-        w_stage = ctx.enter_context(tc.tile_pool(name="w_stage", bufs=3))
+        w_stage = ctx.enter_context(tc.tile_pool(name="w_stage", bufs=5))
         w_quant = ctx.enter_context(tc.tile_pool(name="w_quant", bufs=3))
         psum = ctx.enter_context(tc.psum_pool(name="psum", bufs=8))
 
@@ -102,7 +103,7 @@ def tile_linear_retention_pb_k_kernel(tc, ret_w, kv_h, Wo, bo, grad_out, out):
                     in_=grouped[:, s * K_PASS : (s + 1) * K_PASS],
                 )
 
-        waiting = None
+        waiting = []
         for w in range(WIDTH):
             words = g_raw[w][:].bitcast(F32)
             for pair in range(PASSES // 2):
@@ -117,10 +118,9 @@ def tile_linear_retention_pb_k_kernel(tc, ret_w, kv_h, Wo, bo, grad_out, out):
                     grouped[:].bitcast(F32).rearrange("p (s h u) -> p s h u", s=2, u=2),
                     bank[:].rearrange("p s u h -> p s h u"),
                 )
-                if waiting is not None:
-                    quantise_g(*waiting)
-                waiting = (w, pair, grouped)
-        quantise_g(*waiting)
+                if waiting and (w, pair) < (WIDTH - 1, PASSES // 2 - LATE_PAIRS + 1):
+                    quantise_g(*waiting.pop(0))
+                waiting.append((w, pair, grouped))
 
         acc = [psum.tile([P, TOKENS], F32, name="acc%d" % n, tag="bank") for n in range(HEADS)]
 
@@ -128,19 +128,17 @@ def tile_linear_retention_pb_k_kernel(tc, ret_w, kv_h, Wo, bo, grad_out, out):
         w_codes = {}
         w_scales = {}
 
-        def regroup_w(c):
-            grouped = w_stage.tile([P, KD, PACK], BF16, name="w_grouped%d" % c, tag="w_grouped", align_bytes=64)
-            for use_vector, cols in (
-                (False, slice(VECTOR_COLS, HALF)),
-                (True, slice(0, VECTOR_COLS)),
-                (False, slice(HALF, KD)),
-            ):
+        def regroup_w(c, half):
+            grouped = w_stage.tile(
+                [P, HALF, PACK], BF16, name="w_grouped%d_%d" % (c, half), tag="w_grouped", align_bytes=64
+            )
+            for use_vector, first, last in ((True, 0, VECTOR_COLS), (False, VECTOR_COLS, HALF)):
                 copy_on(
                     use_vector,
-                    grouped[:, cols, :].rearrange("q (c i) t -> q c t i", i=4),
-                    w_raw[c][:, :, cols].rearrange("q t (c i) -> q c t i", i=4),
+                    grouped[:, first:last, :].rearrange("q (c i) t -> q c t i", i=4),
+                    w_raw[c][:, :, half * HALF + first : half * HALF + last].rearrange("q t (c i) -> q c t i", i=4),
                 )
-            w_grouped[c] = grouped
+            w_grouped[c, half] = grouped
 
         def quantise_w(c, half):
             if half == 0:
@@ -150,7 +148,7 @@ def tile_linear_retention_pb_k_kernel(tc, ret_w, kv_h, Wo, bo, grad_out, out):
             nc.vector.quantize_mx(
                 out=w_codes[c][:, cols].bitcast(E4M3_X4),
                 scales=w_scales[c][:, cols],
-                in_=w_grouped[c][:, cols, :].rearrange("q c t -> q (c t)"),
+                in_=w_grouped[c, half][:].rearrange("q c t -> q (c t)"),
             )
 
         def multiply(c, half):
@@ -167,14 +165,17 @@ def tile_linear_retention_pb_k_kernel(tc, ret_w, kv_h, Wo, bo, grad_out, out):
                 )
 
         for c in range(PASSES):
-            regroup_w(c)
-            if c + W_AHEAD < PASSES:
-                load_w(c + W_AHEAD)
+            regroup_w(c, 0)
+            while waiting:
+                quantise_g(*waiting.pop(0))
             if c > 0:
                 quantise_w(c - 1, 1)
                 multiply(c - 1, 1)
             quantise_w(c, 0)
             multiply(c, 0)
+            regroup_w(c, 1)
+            if c + W_AHEAD < PASSES:
+                load_w(c + W_AHEAD)
         quantise_w(PASSES - 1, 1)
         multiply(PASSES - 1, 1)
 

@@ -78,18 +78,19 @@ def tile_linear_retention_pb_k_kernel(tc, ret_w, kv_h, Wo, bo, grad_out, out):
         ident_bf16 = keep.tile([P, P], BF16)
         make_identity(nc, ident_bf16[:])
 
-        kv_t = keep.tile([P, P, KV_ROWS], F32)
+        kv_wide = keep.tile([P, WIDTH, P // 2 // WIDTH, KV_ROWS], F32)
+        kv_narrow = keep.tile([P, WIDTH, P // 2 // WIDTH, KV_ROWS], BF16)
         kv_per_bank = 8
         for b in range(KV_ROWS // kv_per_bank):
             kv_bank = psum.tile([P, kv_per_bank, P], BF16, tag="bank")
             for j in range(kv_per_bank):
                 nc.tensor.transpose(kv_bank[:, j, :], kv_raw[:, b * kv_per_bank + j, :], ident_bf16[:])
-            copy_on(
-                b % 2 == 1,
-                kv_t[:, :, b * kv_per_bank : (b + 1) * kv_per_bank],
-                kv_bank[:].rearrange("f j p -> f p j"),
-            )
-        kv_cols = kv_t[:].rearrange("f p i -> f (p i)")
+            turned = kv_bank[:].rearrange("f j (w r) -> f w r j", w=WIDTH)
+            rows = slice(b * kv_per_bank, (b + 1) * kv_per_bank)
+            middle = P // 2 // WIDTH
+            copy_on(b % 2 == 1, kv_wide[:, :, :, rows], turned[:, :, :middle, :])
+            copy_on(b % 2 == 1, kv_narrow[:, :, :, rows], turned[:, :, middle:, :])
+        kv_cols = [t[:].rearrange("f w r i -> f (w r i)") for t in (kv_wide, kv_narrow)]
 
         g_codes = keep.tile([P, PASSES, TOKENS], U32, align_bytes=64)
         g_scales = keep.tile([P, PASSES, TOKENS], U8, align_bytes=64)
@@ -179,24 +180,43 @@ def tile_linear_retention_pb_k_kernel(tc, ret_w, kv_h, Wo, bo, grad_out, out):
         quantise_w(PASSES - 1, 1)
         multiply(PASSES - 1, 1)
 
-        go2_t = big.tile([P, HEADS, TOKENS], F32, tag="big")
-        for n in range(HEADS):
+        half = HEADS // 2
+        go2_t = big.tile([P, half, TOKENS], F32, tag="big")
+        rest = big.tile([P, half, TOKENS], F32, tag="big")
+        terms = big.tile([P, 3, half, TOKENS], BF16, tag="big")
+        out_sb = big.tile([P, WIDTH, KD], F32, tag="big")
+        for n in range(half):
             copy_on(n % 2 == 1, go2_t[:, n, :], acc[n][:])
 
-        out_sb = big.tile([P, WIDTH, KD], F32, tag="big")
-        heads_per_bank = BANK_F32 // D
-        for b in range(HEADS // heads_per_bank):
+        def split(n, step):
+            high, middle, low = (terms[:, i, n, :] for i in range(3))
+            if step == 0:
+                nc.scalar.copy(out=high, in_=acc[half + n][:])
+                nc.vector.tensor_sub(out=rest[:, n, :], in0=acc[half + n][:], in1=high)
+            else:
+                nc.scalar.copy(out=middle, in_=rest[:, n, :])
+                nc.vector.tensor_sub(out=low, in0=rest[:, n, :], in1=middle)
+
+        for n in range(half + 1):
+            if n < half:
+                split(n, 0)
+            if n > 0:
+                split(n - 1, 1)
+
+        for b in range(2):
             for w in range(WIDTH):
-                out_bank = psum.tile([P, heads_per_bank, D], F32, tag="bank")
-                for j in range(heads_per_bank):
-                    n = b * heads_per_bank + j
-                    nc.tensor.matmul(
-                        out=out_bank[:, j, :],
-                        lhsT=go2_t[:, n, w * HEIGHT : (w + 1) * HEIGHT],
-                        rhs=kv_cols[:, (w * HEADS + n) * D : (w * HEADS + n + 1) * D],
-                        start=True,
-                        stop=True,
-                    )
+                out_bank = psum.tile([P, half, D], F32, tag="bank")
+                tokens = slice(w * HEIGHT, (w + 1) * HEIGHT)
+                for n in range(half):
+                    operands = [go2_t[:, n, tokens]] if b == 0 else [terms[:, i, n, tokens] for i in range(3)]
+                    for i, go2 in enumerate(operands):
+                        nc.tensor.matmul(
+                            out=out_bank[:, n, :],
+                            lhsT=go2,
+                            rhs=kv_cols[b][:, (w * half + n) * D : (w * half + n + 1) * D],
+                            start=(i == 0),
+                            stop=(i == len(operands) - 1),
+                        )
                 cols = slice(b * BANK_F32, (b + 1) * BANK_F32)
                 copy_on(w % 2 == 1, out_sb[:, w, cols], out_bank[:].rearrange("h n e -> h (n e)"))
                 nc.sync.dma_start(out=out_rows[:, w, cols], in_=out_sb[:, w, cols])

@@ -24,6 +24,7 @@ W_AHEAD = 6
 G_PIECES = (2, 2, 2, 4)
 HALF = KD // 2
 VECTOR_COLS = 240
+WIDE = 5
 LATE_PAIRS = 2
 
 FLOPS = 2 * TOKENS * CHANNELS * KD + 2 * WIDTH * HEADS * HEIGHT * D * D
@@ -78,8 +79,9 @@ def tile_linear_retention_pb_k_kernel(tc, ret_w, kv_h, Wo, bo, grad_out, out):
         ident_bf16 = keep.tile([P, P], BF16)
         make_identity(nc, ident_bf16[:])
 
-        kv_wide = keep.tile([P, WIDTH, P // 2 // WIDTH, KV_ROWS], F32)
-        kv_narrow = keep.tile([P, WIDTH, P // 2 // WIDTH, KV_ROWS], BF16)
+        wide_rows = WIDE * D // KV_ROWS
+        kv_wide = keep.tile([P, WIDTH, wide_rows, KV_ROWS], F32)
+        kv_narrow = keep.tile([P, WIDTH, P // WIDTH - wide_rows, KV_ROWS], BF16)
         kv_per_bank = 8
         for b in range(KV_ROWS // kv_per_bank):
             kv_bank = psum.tile([P, kv_per_bank, P], BF16, tag="bank")
@@ -87,10 +89,10 @@ def tile_linear_retention_pb_k_kernel(tc, ret_w, kv_h, Wo, bo, grad_out, out):
                 nc.tensor.transpose(kv_bank[:, j, :], kv_raw[:, b * kv_per_bank + j, :], ident_bf16[:])
             turned = kv_bank[:].rearrange("f j (w r) -> f w r j", w=WIDTH)
             rows = slice(b * kv_per_bank, (b + 1) * kv_per_bank)
-            middle = P // 2 // WIDTH
-            copy_on(b % 2 == 1, kv_wide[:, :, :, rows], turned[:, :, :middle, :])
-            copy_on(b % 2 == 1, kv_narrow[:, :, :, rows], turned[:, :, middle:, :])
-        kv_cols = [t[:].rearrange("f w r i -> f (w r i)") for t in (kv_wide, kv_narrow)]
+            copy_on(b % 2 == 1, kv_wide[:, :, :, rows], turned[:, :, :wide_rows, :])
+            copy_on(b % 2 == 1, kv_narrow[:, :, :, rows], turned[:, :, wide_rows:, :])
+        wide_cols = kv_wide[:].rearrange("f w r i -> f w (r i)")
+        narrow_cols = kv_narrow[:].rearrange("f w r i -> f w (r i)")
 
         g_codes = keep.tile([P, PASSES, TOKENS], U32, align_bytes=64)
         g_scales = keep.tile([P, PASSES, TOKENS], U8, align_bytes=64)
@@ -180,43 +182,41 @@ def tile_linear_retention_pb_k_kernel(tc, ret_w, kv_h, Wo, bo, grad_out, out):
         quantise_w(PASSES - 1, 1)
         multiply(PASSES - 1, 1)
 
-        half = HEADS // 2
-        go2_t = big.tile([P, half, TOKENS], F32, tag="big")
-        rest = big.tile([P, half, TOKENS], F32, tag="big")
-        terms = big.tile([P, 3, half, TOKENS], BF16, tag="big")
+        go2_t = big.tile([P, WIDE, TOKENS], F32, tag="big")
+        rest = big.tile([P, HEADS - WIDE, TOKENS], F32, tag="big")
+        terms = big.tile([P, 3, HEADS - WIDE, TOKENS], BF16, tag="big")
         out_sb = big.tile([P, WIDTH, KD], F32, tag="big")
-        for n in range(half):
+        for n in range(WIDE):
             copy_on(n % 2 == 1, go2_t[:, n, :], acc[n][:])
 
         def split(n, step):
-            high, middle, low = (terms[:, i, n, :] for i in range(3))
+            high, middle, low = (terms[:, i, n - WIDE, :] for i in range(3))
             if step == 0:
-                nc.scalar.copy(out=high, in_=acc[half + n][:])
-                nc.vector.tensor_sub(out=rest[:, n, :], in0=acc[half + n][:], in1=high)
+                nc.scalar.copy(out=high, in_=acc[n][:])
+                nc.vector.tensor_sub(out=rest[:, n - WIDE, :], in0=acc[n][:], in1=high)
             else:
-                nc.scalar.copy(out=middle, in_=rest[:, n, :])
-                nc.vector.tensor_sub(out=low, in0=rest[:, n, :], in1=middle)
+                nc.scalar.copy(out=middle, in_=rest[:, n - WIDE, :])
+                nc.vector.tensor_sub(out=low, in0=rest[:, n - WIDE, :], in1=middle)
 
-        for n in range(half + 1):
-            if n < half:
-                split(n, 0)
-            if n > 0:
-                split(n - 1, 1)
+        for step in range(2):
+            for n in range(WIDE, HEADS):
+                split(n, step)
+        def second(n, w, dst):
+            tokens = slice(w * HEIGHT, (w + 1) * HEIGHT)
+            if n < WIDE:
+                pairs = [(go2_t[:, n, tokens], wide_cols[:, w, n * D : (n + 1) * D])]
+            else:
+                kv_n = narrow_cols[:, w, (n - WIDE) * D : (n - WIDE + 1) * D]
+                pairs = [(terms[:, i, n - WIDE, tokens], kv_n) for i in range(3)]
+            for i, (go2, kv_n) in enumerate(pairs):
+                nc.tensor.matmul(out=dst, lhsT=go2, rhs=kv_n, start=(i == 0), stop=(i == len(pairs) - 1))
 
-        for b in range(2):
-            for w in range(WIDTH):
-                out_bank = psum.tile([P, half, D], F32, tag="bank")
-                tokens = slice(w * HEIGHT, (w + 1) * HEIGHT)
-                for n in range(half):
-                    operands = [go2_t[:, n, tokens]] if b == 0 else [terms[:, i, n, tokens] for i in range(3)]
-                    for i, go2 in enumerate(operands):
-                        nc.tensor.matmul(
-                            out=out_bank[:, n, :],
-                            lhsT=go2,
-                            rhs=kv_cols[b][:, (w * half + n) * D : (w * half + n + 1) * D],
-                            start=(i == 0),
-                            stop=(i == len(operands) - 1),
-                        )
-                cols = slice(b * BANK_F32, (b + 1) * BANK_F32)
-                copy_on(w % 2 == 1, out_sb[:, w, cols], out_bank[:].rearrange("h n e -> h (n e)"))
-                nc.sync.dma_start(out=out_rows[:, w, cols], in_=out_sb[:, w, cols])
+        banks = [(w, range(4)) for w in range(WIDTH)] + [(w, range(4, HEADS)) for w in range(WIDTH - 1)]
+        banks += [(WIDTH - 1, range(4, 6)), (WIDTH - 1, range(6, HEADS))]
+        for i, (w, heads) in enumerate(banks):
+            out_bank = psum.tile([P, len(heads), D], F32, name="out_bank%d" % i, tag="bank")
+            for j, n in enumerate(heads):
+                second(n, w, out_bank[:, j, :])
+            cols = slice(heads[0] * D, (heads[-1] + 1) * D)
+            copy_on(i % 2 == 1, out_sb[:, w, cols], out_bank[:].rearrange("h n e -> h (n e)"))
+            nc.sync.dma_start(out=out_rows[:, w, cols], in_=out_sb[:, w, cols])

@@ -22,9 +22,8 @@ BANK_F32 = 512
 KV_ROWS = 32
 W_AHEAD = 6
 G_PIECES = (2, 2, 2, 4)
-HALF = KD // 2
-VECTOR_COLS = 240
-WIDE = 5
+VECTOR_PART, VECTOR_OF = 15, 32
+WIDE = 4
 LATE_PAIRS = 2
 
 FLOPS = 2 * TOKENS * CHANNELS * KD + 2 * WIDTH * HEADS * HEIGHT * D * D
@@ -117,7 +116,7 @@ def tile_linear_retention_pb_k_kernel(tc, ret_w, kv_h, Wo, bo, grad_out, out):
                         nc.tensor.transpose(bank[:, s, u, :], words[:, first : first + P], ident_f32[:])
                 grouped = g_stage.tile([P, 2 * K_PASS], BF16, align_bytes=64)
                 copy_on(
-                    pair % 4 == 3,
+                    pair % 4 == 3 and (w, pair) != (WIDTH - 1, PASSES // 2 - 1),
                     grouped[:].bitcast(F32).rearrange("p (s h u) -> p s h u", s=2, u=2),
                     bank[:].rearrange("p s u h -> p s h u"),
                 )
@@ -126,36 +125,35 @@ def tile_linear_retention_pb_k_kernel(tc, ret_w, kv_h, Wo, bo, grad_out, out):
                 waiting.append((w, pair, grouped))
 
         acc = [psum.tile([P, TOKENS], F32, name="acc%d" % n, tag="bank") for n in range(HEADS)]
-
         w_grouped = {}
         w_codes = {}
         w_scales = {}
 
-        def regroup_w(c, half):
+        def regroup_w(c, first, last):
             grouped = w_stage.tile(
-                [P, HALF, PACK], BF16, name="w_grouped%d_%d" % (c, half), tag="w_grouped", align_bytes=64
+                [P, last - first, PACK], BF16, name="w_grouped%d_%d" % (c, first), tag="w_grouped", align_bytes=64
             )
-            for use_vector, first, last in ((True, 0, VECTOR_COLS), (False, VECTOR_COLS, HALF)):
+            middle = first + (last - first) * VECTOR_PART // VECTOR_OF
+            for use_vector, lo, hi in ((True, first, middle), (False, middle, last)):
                 copy_on(
                     use_vector,
-                    grouped[:, first:last, :].rearrange("q (c i) t -> q c t i", i=4),
-                    w_raw[c][:, :, half * HALF + first : half * HALF + last].rearrange("q t (c i) -> q c t i", i=4),
+                    grouped[:, lo - first : hi - first, :].rearrange("q (c i) t -> q c t i", i=4),
+                    w_raw[c][:, :, lo:hi].rearrange("q t (c i) -> q c t i", i=4),
                 )
-            w_grouped[c, half] = grouped
+            w_grouped[c, first] = grouped
 
-        def quantise_w(c, half):
-            if half == 0:
+        def quantise_w(c, first, last):
+            if first == 0:
                 w_codes[c] = w_quant.tile([P, KD], U32, name="w_codes%d" % c, tag="w_codes", align_bytes=64)
                 w_scales[c] = w_quant.tile([P, KD], U8, name="w_scales%d" % c, tag="w_scales", align_bytes=64)
-            cols = slice(half * HALF, (half + 1) * HALF)
             nc.vector.quantize_mx(
-                out=w_codes[c][:, cols].bitcast(E4M3_X4),
-                scales=w_scales[c][:, cols],
-                in_=w_grouped[c, half][:].rearrange("q c t -> q (c t)"),
+                out=w_codes[c][:, first:last].bitcast(E4M3_X4),
+                scales=w_scales[c][:, first:last],
+                in_=w_grouped[c, first][:].rearrange("q c t -> q (c t)"),
             )
 
-        def multiply(c, half):
-            for n in range(half * HEADS // 2, (half + 1) * HEADS // 2):
+        def multiply(c, first, last):
+            for n in range(first // D, last // D):
                 cols = slice(n * D, (n + 1) * D)
                 nc.tensor.matmul_mx(
                     out=acc[n][:],
@@ -167,20 +165,22 @@ def tile_linear_retention_pb_k_kernel(tc, ret_w, kv_h, Wo, bo, grad_out, out):
                     stop=(c == PASSES - 1),
                 )
 
+        units = []
         for c in range(PASSES):
-            regroup_w(c, 0)
+            width = KD // 4 if c in (0, PASSES - 1) else KD // 2
+            units += [(c, first, first + width) for first in range(0, KD, width)]
+        for i, unit in enumerate(units):
+            regroup_w(*unit)
+            c, first, last = unit
+            if last == KD and c + W_AHEAD < PASSES:
+                load_w(c + W_AHEAD)
             while waiting:
                 quantise_g(*waiting.pop(0))
-            if c > 0:
-                quantise_w(c - 1, 1)
-                multiply(c - 1, 1)
-            quantise_w(c, 0)
-            multiply(c, 0)
-            regroup_w(c, 1)
-            if c + W_AHEAD < PASSES:
-                load_w(c + W_AHEAD)
-        quantise_w(PASSES - 1, 1)
-        multiply(PASSES - 1, 1)
+            if i > 0:
+                quantise_w(*units[i - 1])
+                multiply(*units[i - 1])
+        quantise_w(*units[-1])
+        multiply(*units[-1])
 
         go2_t = big.tile([P, WIDE, TOKENS], F32, tag="big")
         rest = big.tile([P, HEADS - WIDE, TOKENS], F32, tag="big")
@@ -211,8 +211,8 @@ def tile_linear_retention_pb_k_kernel(tc, ret_w, kv_h, Wo, bo, grad_out, out):
             for i, (go2, kv_n) in enumerate(pairs):
                 nc.tensor.matmul(out=dst, lhsT=go2, rhs=kv_n, start=(i == 0), stop=(i == len(pairs) - 1))
 
-        banks = [(w, range(4)) for w in range(WIDTH)] + [(w, range(4, HEADS)) for w in range(WIDTH - 1)]
-        banks += [(WIDTH - 1, range(4, 6)), (WIDTH - 1, range(6, HEADS))]
+        banks = [(w, range(WIDE)) for w in range(WIDTH)] + [(w, range(WIDE, HEADS)) for w in range(WIDTH - 1)]
+        banks += [(WIDTH - 1, heads) for heads in (range(WIDE, 6), range(6, 7), range(7, HEADS))]
         for i, (w, heads) in enumerate(banks):
             out_bank = psum.tile([P, len(heads), D], F32, name="out_bank%d" % i, tag="bank")
             for j, n in enumerate(heads):

from contextlib import ExitStack

import concourse.mybir as mybir
from concourse.masks import make_identity

F32 = mybir.dt.float32
BF16 = mybir.dt.bfloat16
U32 = mybir.dt.uint32
U8 = mybir.dt.uint8
E4M3_X4 = mybir.dt.float8_e4m3fn_x4
E5M2_X4 = mybir.dt.float8_e5m2_x4

P = 128
PACK = 4
K_PASS = P * PACK
HEIGHT, WIDTH, HEADS, D = 128, 4, 8, 128
TOKENS = HEIGHT * WIDTH
CHANNELS = 8192
KD = HEADS * D
PASSES = CHANNELS // K_PASS
BANK_F32 = 512
KV_ROWS = 32
W_AHEAD = 6
G_PIECES = (2, 2, 2, 4)
VECTOR_PART, VECTOR_OF = 15, 32
WIDE = 4
LATE_PAIRS = 2

FLOPS = 2 * TOKENS * CHANNELS * KD + 2 * WIDTH * HEADS * HEIGHT * D * D


def tile_linear_retention_pb_k_kernel(tc, ret_w, kv_h, Wo, bo, grad_out, out):
    nc = tc.nc

    g_tiles = grad_out.rearrange("b (h w) k -> (b w) h k", w=WIDTH)
    w_passes = Wo.rearrange("(g u q e) c -> g q u (e c)", u=2, q=P, e=2)
    kv_rows = kv_h.rearrange("b w n (a i) f -> (b w n a) i f", i=KV_ROWS)
    out_rows = out.rearrange("b h w n e -> (b h) w (n e)")

    def copy_on(use_vector, dst, src):
        if use_vector:
            nc.vector.tensor_copy(out=dst, in_=src)
        else:
            nc.scalar.copy(out=dst, in_=src)

    with ExitStack() as ctx:
        ctx.enter_context(tc.manual_schedule())
        keep = ctx.enter_context(tc.tile_pool(name="keep", bufs=1))
        big = ctx.enter_context(tc.tile_pool(name="big", bufs=WIDTH))
        w_in = ctx.enter_context(tc.tile_pool(name="w_in", bufs=W_AHEAD))
        g_stage = ctx.enter_context(tc.tile_pool(name="g_stage", bufs=5))
        w_stage = ctx.enter_context(tc.tile_pool(name="w_stage", bufs=5))
        w_quant = ctx.enter_context(tc.tile_pool(name="w_quant", bufs=3))
        psum = ctx.enter_context(tc.psum_pool(name="psum", bufs=8))

        kv_raw = keep.tile([P, KV_ROWS, D], BF16)
        nc.sync.dma_start(out=kv_raw[:], in_=kv_rows)
        g_raw = []
        for w in range(WIDTH):
            g_raw.append(big.tile([P, CHANNELS], BF16, name="g_raw%d" % w, tag="big"))
            for piece in range(G_PIECES[w]):
                cols = slice(piece * CHANNELS // G_PIECES[w], (piece + 1) * CHANNELS // G_PIECES[w])
                nc.sync.dma_start(out=g_raw[w][:, cols], in_=g_tiles[w, :, cols])

        w_raw = {}

        def load_w(c):
            w_raw[c] = w_in.tile([P, PACK, KD], BF16, name="w_raw%d" % c, tag="w_raw")
            nc.sync.dma_start(
                out=w_raw[c][:].rearrange("q (u e) c -> q u (e c)", u=2), in_=w_passes[c, :, :, :]
            )

        for c in range(W_AHEAD):
            load_w(c)

        ident_f32 = keep.tile([P, P], F32)
        make_identity(nc, ident_f32[:])
        ident_bf16 = keep.tile([P, P], BF16)
        make_identity(nc, ident_bf16[:])

        wide_rows = WIDE * D // KV_ROWS
        kv_wide = keep.tile([P, WIDTH, wide_rows, KV_ROWS], F32)
        kv_narrow = keep.tile([P, WIDTH, P // WIDTH - wide_rows, KV_ROWS], BF16)
        kv_per_bank = 8
        for b in range(KV_ROWS // kv_per_bank):
            kv_bank = psum.tile([P, kv_per_bank, P], BF16, tag="bank")
            for j in range(kv_per_bank):
                nc.tensor.transpose(kv_bank[:, j, :], kv_raw[:, b * kv_per_bank + j, :], ident_bf16[:])
            turned = kv_bank[:].rearrange("f j (w r) -> f w r j", w=WIDTH)
            rows = slice(b * kv_per_bank, (b + 1) * kv_per_bank)
            copy_on(b % 2 == 1, kv_wide[:, :, :, rows], turned[:, :, :wide_rows, :])
            copy_on(b % 2 == 1, kv_narrow[:, :, :, rows], turned[:, :, wide_rows:, :])
        wide_cols = kv_wide[:].rearrange("f w r i -> f w (r i)")
        narrow_cols = kv_narrow[:].rearrange("f w r i -> f w (r i)")

        g_codes = keep.tile([P, PASSES, TOKENS], U32, align_bytes=64)
        g_scales = keep.tile([P, PASSES, TOKENS], U8, align_bytes=64)

        def quantise_g(w, pair, grouped):
            for s in range(2):
                g = 2 * pair + s
                nc.vector.quantize_mx(
                    out=g_codes[:, g, w * P : (w + 1) * P].bitcast(E5M2_X4),
                    scales=g_scales[:, g, w * P : (w + 1) * P],
                    in_=grouped[:, s * K_PASS : (s + 1) * K_PASS],
                )

        waiting = []
        for w in range(WIDTH):
            words = g_raw[w][:].bitcast(F32)
            for pair in range(PASSES // 2):
                bank = psum.tile([P, 2, 2, P], F32, tag="bank")
                for s in range(2):
                    for u in range(2):
                        first = (2 * pair + s) * (K_PASS // 2) + u * P
                        nc.tensor.transpose(bank[:, s, u, :], words[:, first : first + P], ident_f32[:])
                grouped = g_stage.tile([P, 2 * K_PASS], BF16, align_bytes=64)
                copy_on(
                    pair % 4 == 3 and (w, pair) != (WIDTH - 1, PASSES // 2 - 1),
                    grouped[:].bitcast(F32).rearrange("p (s h u) -> p s h u", s=2, u=2),
                    bank[:].rearrange("p s u h -> p s h u"),
                )
                if waiting and (w, pair) < (WIDTH - 1, PASSES // 2 - LATE_PAIRS + 1):
                    quantise_g(*waiting.pop(0))
                waiting.append((w, pair, grouped))

        acc = [psum.tile([P, TOKENS], F32, name="acc%d" % n, tag="bank") for n in range(HEADS)]
        w_grouped = {}
        w_codes = {}
        w_scales = {}

        def regroup_w(c, first, last):
            grouped = w_stage.tile(
                [P, last - first, PACK], BF16, name="w_grouped%d_%d" % (c, first), tag="w_grouped", align_bytes=64
            )
            middle = first + (last - first) * VECTOR_PART // VECTOR_OF
            for use_vector, lo, hi in ((True, first, middle), (False, middle, last)):
                copy_on(
                    use_vector,
                    grouped[:, lo - first : hi - first, :].rearrange("q (c i) t -> q c t i", i=4),
                    w_raw[c][:, :, lo:hi].rearrange("q t (c i) -> q c t i", i=4),
                )
            w_grouped[c, first] = grouped

        def quantise_w(c, first, last):
            if first == 0:
                w_codes[c] = w_quant.tile([P, KD], U32, name="w_codes%d" % c, tag="w_codes", align_bytes=64)
                w_scales[c] = w_quant.tile([P, KD], U8, name="w_scales%d" % c, tag="w_scales", align_bytes=64)
            nc.vector.quantize_mx(
                out=w_codes[c][:, first:last].bitcast(E4M3_X4),
                scales=w_scales[c][:, first:last],
                in_=w_grouped[c, first][:].rearrange("q c t -> q (c t)"),
            )

        def multiply(c, first, last):
            for n in range(first // D, last // D):
                cols = slice(n * D, (n + 1) * D)
                nc.tensor.matmul_mx(
                    out=acc[n][:],
                    lhsT=w_codes[c][:, cols].bitcast(E4M3_X4),
                    lhsT_scale=w_scales[c][:, cols],
                    rhs=g_codes[:, c, :].bitcast(E5M2_X4),
                    rhs_scale=g_scales[:, c, :],
                    start=(c == 0),
                    stop=(c == PASSES - 1),
                )

        units = []
        for c in range(PASSES):
            width = KD // 4 if c in (0, PASSES - 1) else KD // 2
            units += [(c, first, first + width) for first in range(0, KD, width)]
        for i, unit in enumerate(units):
            regroup_w(*unit)
            c, first, last = unit
            if last == KD and c + W_AHEAD < PASSES:
                load_w(c + W_AHEAD)
            while waiting:
                quantise_g(*waiting.pop(0))
            if i > 0:
                quantise_w(*units[i - 1])
                multiply(*units[i - 1])
        quantise_w(*units[-1])
        multiply(*units[-1])

        go2_t = big.tile([P, WIDE, TOKENS], F32, tag="big")
        rest = big.tile([P, HEADS - WIDE, TOKENS], F32, tag="big")
        terms = big.tile([P, 3, HEADS - WIDE, TOKENS], BF16, tag="big")
        out_sb = big.tile([P, WIDTH, KD], F32, tag="big")
        for n in range(WIDE):
            copy_on(n % 2 == 1, go2_t[:, n, :], acc[n][:])

        def split(n, step):
            high, middle, low = (terms[:, i, n - WIDE, :] for i in range(3))
            if step == 0:
                nc.scalar.copy(out=high, in_=acc[n][:])
                nc.vector.tensor_sub(out=rest[:, n - WIDE, :], in0=acc[n][:], in1=high)
            else:
                nc.scalar.copy(out=middle, in_=rest[:, n - WIDE, :])
                nc.vector.tensor_sub(out=low, in0=rest[:, n - WIDE, :], in1=middle)

        for step in range(2):
            for n in range(WIDE, HEADS):
                split(n, step)
        def second(n, w, dst):
            tokens = slice(w * HEIGHT, (w + 1) * HEIGHT)
            if n < WIDE:
                pairs = [(go2_t[:, n, tokens], wide_cols[:, w, n * D : (n + 1) * D])]
            else:
                kv_n = narrow_cols[:, w, (n - WIDE) * D : (n - WIDE + 1) * D]
                pairs = [(terms[:, i, n - WIDE, tokens], kv_n) for i in range(3)]
            for i, (go2, kv_n) in enumerate(pairs):
                nc.tensor.matmul(out=dst, lhsT=go2, rhs=kv_n, start=(i == 0), stop=(i == len(pairs) - 1))

        banks = [(w, range(WIDE)) for w in range(WIDTH)] + [(w, range(WIDE, HEADS)) for w in range(WIDTH - 1)]
        banks += [(WIDTH - 1, heads) for heads in (range(WIDE, 6), range(6, 7), range(7, HEADS))]
        for i, (w, heads) in enumerate(banks):
            out_bank = psum.tile([P, len(heads), D], F32, name="out_bank%d" % i, tag="bank")
            for j, n in enumerate(heads):
                second(n, w, out_bank[:, j, :])
            cols = slice(heads[0] * D, (heads[-1] + 1) * D)
            copy_on(i % 2 == 1, out_sb[:, w, cols], out_bank[:].rearrange("h n e -> h (n e)"))
            nc.sync.dma_start(out=out_rows[:, w, cols], in_=out_sb[:, w, cols])
